import numpy as np
import ml_dtypes


def mxq(x, axis, fmt="e4m3"):
    dtype, down = {"e4m3": (ml_dtypes.float8_e4m3fn, 7), "e5m2": (ml_dtypes.float8_e5m2, 14)}[fmt]
    v = np.moveaxis(np.asarray(x, np.float32).astype(ml_dtypes.bfloat16).astype(np.float64), axis, -1)
    blocks = v.reshape(v.shape[:-1] + (-1, 32))
    amax = np.abs(blocks).max(-1, keepdims=True)
    byte = np.maximum(np.where(amax > 0, np.frexp(amax)[1] - 1 + 127, 0) - down, 1)
    scale = np.exp2(byte - 127.0)
    codes = (blocks / scale).astype(np.float32).astype(dtype).astype(np.float64)
    return np.moveaxis((codes * scale).reshape(v.shape), -1, axis)


WIDE = False


def mx_kscale(k):
    if not WIDE:
        return np.ones(k)
    levels = np.array([10, -10, 5, -5, 0])
    a = np.random.permutation(np.resize(levels, k // 512 * 4)).reshape(k // 512, 4)
    idx = np.arange(k)
    return np.exp2(a[idx // 512, idx % 128 // 32])


BF16 = ml_dtypes.bfloat16


def bf(x):
    return np.asarray(x, np.float32).astype(BF16)


def f64(x):
    return np.asarray(x).astype(np.float64)


B, L, H, D = 8, 512, 4, 128
DIM = H * D


def sigmoid(a):
    return 1.0 / (1.0 + np.exp(-a))


def setup_inputs():
    r = np.random.standard_normal
    s = mx_kscale(DIM)
    return {"q_rot_re": bf(r((B, L, H, D)) * 0.36),
            "q_rot_im": bf(r((B, L, H, D)) * 0.36),
            "k_rot_re": bf(r((B, L, H, D)) * 0.36),
            "k_rot_im": bf(r((B, L, H, D)) * 0.36),
            "x": bf(r((B, L, DIM)) * s),
            "wv_w": bf(r((DIM, DIM)) * 0.5 / np.sqrt(DIM) / s[None, :]),
            "wv_b": bf(r(DIM) * 0.1),
            "amplitude": bf(3.5 + 0.5 * r(H))}


def reference(q_rot_re, q_rot_im, k_rot_re, k_rot_im, x, wv_w, wv_b, amplitude):
    v = (mxq(f64(x), 2, "e4m3") @ mxq(f64(wv_w), 1, "e4m3").T) + f64(wv_b)
    v = v.reshape(B, L, H, D).transpose(0, 2, 1, 3)
    qk_re = (f64(q_rot_re).transpose(0, 2, 1, 3) @ f64(k_rot_re).transpose(0, 2, 3, 1)
             - f64(q_rot_im).transpose(0, 2, 1, 3) @ f64(k_rot_im).transpose(0, 2, 3, 1))
    amp = sigmoid(f64(amplitude))
    t = np.arange(L)
    diff = t[:, None] - t[None, :]
    tril = diff >= 0
    decay = np.where(tril[None], amp[:, None, None] ** np.where(tril, diff, 0)[None], 0.0)
    p = qk_re * decay[None]
    inner = mxq(p, 3, "e4m3") @ mxq(v, 2, "e4m3")
    return inner.transpose(0, 2, 1, 3).reshape(B, L, DIM)

@@ -1,0 +1,247 @@
+from contextlib import ExitStack
+
+import concourse.mybir as mybir
+from concourse.masks import make_identity
+
+BF16 = mybir.dt.bfloat16
+F32 = mybir.dt.float32
+I32 = mybir.dt.int32
+U32 = mybir.dt.uint32
+U8 = mybir.dt.uint8
+FP8X4 = mybir.dt.float8_e4m3fn_x4
+ALU = mybir.AluOpType
+ACT = mybir.ActivationFunctionType
+
+B, L, H, D = 8, 512, 4, 128
+DIM = H * D
+P = 128
+PACK = 4
+TILES = L // P
+UNITS = B * H
+P_RING = 3
+
+FLOPS = 2 * B * L * DIM * DIM + 3 * 2 * B * H * L * L * D
+
+
+def tile_retention_pb_t_kernel(
+    tc, q_rot_re, q_rot_im, k_rot_re, k_rot_im, x, wv_w, wv_b, amplitude, out
+):
+    nc = tc.nc
+    with ExitStack() as ctx:
+        const = ctx.enter_context(tc.tile_pool(name="const", bufs=1))
+        inputs = ctx.enter_context(tc.tile_pool(name="inputs", bufs=3))
+        work = ctx.enter_context(tc.tile_pool(name="work", bufs=2))
+        psum = ctx.enter_context(tc.psum_pool(name="psum", bufs=1))
+
+        def load_rows(name, rows):
+            sb = inputs.tile([P, TILES * DIM], BF16, name=name, tag=name)
+            nc.sync.dma_start(
+                out=sb[:].rearrange("p (i c) -> p i c", i=TILES),
+                in_=rows.rearrange("(i p) c -> p i c", p=P),
+            )
+            return sb
+
+        def load_batch(b):
+            return {
+                "x": load_rows("x_sb", x[b]),
+                "k_re": load_rows("k_re_sb", k_rot_re[b].rearrange("l h d -> l (h d)")),
+                "k_im": load_rows("k_im_sb", k_rot_im[b].rearrange("l h d -> l (h d)")),
+                "q_re": load_rows("q_re_sb", q_rot_re[b].rearrange("l h d -> l (h d)")),
+                "q_im": load_rows("q_im_sb", q_rot_im[b].rearrange("l h d -> l (h d)")),
+            }
+
+        w_sb = const.tile([P, TILES * DIM], BF16)
+        nc.sync.dma_start(
+            out=w_sb[:].rearrange("p (i c) -> p i c", i=TILES),
+            in_=wv_w.rearrange("(i p) c -> p i c", p=P),
+        )
+        loaded = {0: load_batch(0), 1: load_batch(1)}
+        amp_logit = const.tile([P, H], BF16)
+        nc.scalar.dma_start(out=amp_logit[:], in_=amplitude.partition_broadcast(P))
+        bias = const.tile([P, DIM], BF16)
+        nc.scalar.dma_start(out=bias[:], in_=wv_b.partition_broadcast(P))
+
+        ident_bf16 = const.tile([P, P], BF16)
+        make_identity(nc, ident_bf16[:])
+        ident_f32 = const.tile([P, P], F32)
+        make_identity(nc, ident_f32[:])
+
+        p_grouped = [
+            const.tile([P, TILES, P, PACK], BF16, name="p_grouped%d" % r, align_bytes=64)
+            for r in range(P_RING)
+        ]
+        for r in range(P_RING):
+            nc.vector.memset(p_grouped[r][:], 0.0)
+
+        distance_i32 = const.tile([P, P, PACK], I32)
+        nc.gpsimd.iota(
+            distance_i32[:], pattern=[[1, P], [-P, PACK]], base=3 * P, channel_multiplier=-1
+        )
+        distance = const.tile([P, P, PACK], F32)
+        nc.vector.tensor_copy(out=distance[:], in_=distance_i32[:])
+        causal = const.tile([P, P, PACK], F32)
+        nc.vector.tensor_single_scalar(out=causal[:], in_=distance[:], scalar=0.0, op=ALU.is_ge)
+        nc.vector.tensor_scalar_max(out=distance[:], in0=distance[:], scalar1=0.0)
+        amp = const.tile([P, H], F32)
+        nc.scalar.activation(out=amp[:], in_=amp_logit[:], func=ACT.Sigmoid)
+        log_amp = const.tile([P, H], F32)
+        nc.scalar.activation(out=log_amp[:], in_=amp[:], func=ACT.Ln)
+        decay = []
+        for h in range(H):
+            decay_h = const.tile([P, P, PACK], F32, name="decay%d" % h)
+            nc.vector.tensor_scalar_mul(
+                out=decay_h[:], in0=distance[:], scalar1=log_amp[:, h : h + 1]
+            )
+            nc.scalar.activation(out=decay_h[:], in_=decay_h[:], func=ACT.Exp)
+            nc.vector.tensor_mul(out=decay_h[:], in0=decay_h[:], in1=causal[:])
+            decay.append(decay_h)
+
+        def quantise_channels_last(rows_sb, name):
+            words = rows_sb[:].bitcast(F32)
+            grouped = work.tile([P, L * PACK], BF16, name=name + "_grouped", align_bytes=64)
+            grouped_words = grouped[:].bitcast(F32).rearrange("p (r u) -> p r u", u=2)
+            for half in range(2):
+                flipped = psum.tile([P, 2, 2 * P], F32, name="flipped_words")
+                for i in range(2):
+                    for u in range(2):
+                        first = (2 * half + i) * 2 * P + u * P
+                        nc.tensor.transpose(
+                            flipped[:, u, i * P : (i + 1) * P],
+                            words[:, first : first + P],
+                            ident_f32[:],
+                        )
+                nc.scalar.copy(
+                    out=grouped_words[:, half * 2 * P : (half + 1) * 2 * P, :],
+                    in_=flipped[:].rearrange("p u r -> p r u"),
+                )
+            codes = work.tile([P, L], U32, name=name + "_codes", align_bytes=64)
+            scales = work.tile([P, L], U8, name=name + "_scales", align_bytes=64)
+            nc.vector.quantize_mx(out=codes[:].bitcast(FP8X4), scales=scales[:], in_=grouped[:])
+            return codes, scales
+
+        w_codes, w_scales = quantise_channels_last(w_sb, "w")
+
+        def project_values(x_codes, x_scales):
+            v_grouped = work.tile([P, H, D, PACK], BF16, align_bytes=64)
+            for h in range(H):
+                v_acc = psum.tile([P, TILES, D], F32)
+                for t in range(TILES):
+                    nc.tensor.matmul_mx(
+                        out=v_acc[:, t, :],
+                        lhsT=x_codes[:, t * P : (t + 1) * P].bitcast(FP8X4),
+                        lhsT_scale=x_scales[:, t * P : (t + 1) * P],
+                        rhs=w_codes[:, h * D : (h + 1) * D].bitcast(FP8X4),
+                        rhs_scale=w_scales[:, h * D : (h + 1) * D],
+                        start=True,
+                        stop=True,
+                    )
+                nc.vector.tensor_tensor(
+                    out=v_grouped[:, h, :, :],
+                    in0=v_acc[:].rearrange("p t d -> p d t"),
+                    in1=bias[:, h * D : (h + 1) * D].unsqueeze(2).to_broadcast([P, D, PACK]),
+                    op=ALU.add,
+                )
+            v_codes = work.tile([P, DIM], U32, align_bytes=64)
+            v_scales = work.tile([P, DIM], U8, align_bytes=64)
+            nc.vector.quantize_mx(
+                out=v_codes[:].bitcast(FP8X4),
+                scales=v_scales[:],
+                in_=v_grouped[:].rearrange("p h d t -> p (h d t)"),
+            )
+            return v_codes, v_scales
+
+        def flip_head(batch_sb, h):
+            flipped = {}
+            for who in ("q", "k"):
+                bank = psum.tile([P, 2, L], BF16, name="flipped_qk", bufs=2)
+                for c, part in enumerate(("re", "im")):
+                    rows_sb = batch_sb[who + "_" + part]
+                    for i in range(TILES):
+                        first = i * DIM + h * D
+                        nc.tensor.transpose(
+                            bank[:, c, i * P : (i + 1) * P],
+                            rows_sb[:, first : first + D],
+                            ident_bf16[:],
+                        )
+                flipped[who] = bank
+            q_t = work.tile([P, 2, L], BF16)
+            nc.scalar.copy(out=q_t[:], in_=flipped["q"][:])
+            k_t = work.tile([P, 2, L], BF16)
+            nc.scalar.copy(out=k_t[:, 0, :], in_=flipped["k"][:, 0, :])
+            nc.scalar.mul(out=k_t[:, 1, :], in_=flipped["k"][:, 1, :], mul=-1.0)
+            return q_t, k_t
+
+        def decayed_scores(unit, q_t, k_t):
+            h = unit % H
+            grouped = p_grouped[unit % P_RING]
+            for i in range(TILES):
+                keys = i + 1
+                scores = psum.tile([P, TILES, P], F32, bufs=3)
+                for t in range(keys):
+                    for c in range(2):
+                        nc.tensor.matmul(
+                            out=scores[:, t, :],
+                            lhsT=k_t[:, c, t * P : (t + 1) * P],
+                            rhs=q_t[:, c, i * P : (i + 1) * P],
+                            start=(c == 0),
+                            stop=(c == 1),
+                        )
+                nc.vector.tensor_tensor(
+                    out=grouped[:, i, :, 0:keys],
+                    in0=scores[:, 0:keys, :].rearrange("p t j -> p j t"),
+                    in1=decay[h][:, :, PACK - keys : PACK],
+                    op=ALU.mult,
+                )
+            p_codes = work.tile([P, L], U32, align_bytes=64)
+            p_scales = work.tile([P, L], U8, align_bytes=64)
+            nc.vector.quantize_mx(
+                out=p_codes[:].bitcast(FP8X4),
+                scales=p_scales[:],
+                in_=grouped[:].rearrange("p i j t -> p (i j t)"),
+            )
+            return p_codes, p_scales
+
+        def weighted_values(h, p_codes, p_scales, v_codes, v_scales, out_sb):
+            o_acc = psum.tile([P, TILES, D], F32)
+            for i in range(TILES):
+                nc.tensor.matmul_mx(
+                    out=o_acc[:, i, :],
+                    lhsT=p_codes[:, i * P : (i + 1) * P].bitcast(FP8X4),
+                    lhsT_scale=p_scales[:, i * P : (i + 1) * P],
+                    rhs=v_codes[:, h * D : (h + 1) * D].bitcast(FP8X4),
+                    rhs_scale=v_scales[:, h * D : (h + 1) * D],
+                    start=True,
+                    stop=True,
+                )
+            nc.scalar.copy(out=out_sb[:, :, h * D : (h + 1) * D], in_=o_acc[:])
+
+        values = {0: project_values(*quantise_channels_last(loaded[0]["x"], "x"))}
+        heads = {0: flip_head(loaded[0], 0)}
+        x_quantised = {}
+        probs = {}
+        out_tiles = {}
+
+        def finish(unit):
+            b, h = divmod(unit, H)
+            if h == 0:
+                out_tiles[b] = work.tile([P, TILES, DIM], F32, name="out_sb")
+            weighted_values(h, *probs[unit], *values[b], out_tiles[b])
+            if h == H - 1:
+                nc.sync.dma_start(
+                    out=out[b].rearrange("(i p) c -> p i c", p=P), in_=out_tiles[b][:]
+                )
+
+        for unit in range(UNITS):
+            b, h = divmod(unit, H)
+            if h == 0 and b + 2 < B:
+                loaded[b + 2] = load_batch(b + 2)
+            if unit + 1 < UNITS:
+                heads[unit + 1] = flip_head(loaded[(unit + 1) // H], (unit + 1) % H)
+            if h == 1 and b + 1 < B:
+                x_quantised[b + 1] = quantise_channels_last(loaded[b + 1]["x"], "x")
+            probs[unit] = decayed_scores(unit, *heads[unit])
+            if h == 2 and b + 1 < B:
+                values[b + 1] = project_values(*x_quantised[b + 1])
+            if unit >= 1:
+                finish(unit - 1)
+        finish(UNITS - 1)

@@ -28,50 +28,45 @@ def tile_retention_pb_t_kernel(
 ):
     nc = tc.nc
     with ExitStack() as ctx:
+        ctx.enter_context(tc.manual_schedule())
         const = ctx.enter_context(tc.tile_pool(name="const", bufs=1))
         inputs = ctx.enter_context(tc.tile_pool(name="inputs", bufs=3))
         work = ctx.enter_context(tc.tile_pool(name="work", bufs=2))
         psum = ctx.enter_context(tc.psum_pool(name="psum", bufs=1))
 
-        def load_rows(name, rows):
-            sb = inputs.tile([P, TILES * DIM], BF16, name=name, tag=name)
+        def load_rows(pool, name, rows):
+            rows_sb = pool.tile([P, TILES * DIM], BF16, name=name)
             nc.sync.dma_start(
-                out=sb[:].rearrange("p (i c) -> p i c", i=TILES),
+                out=rows_sb[:].rearrange("p (i c) -> p i c", i=TILES),
                 in_=rows.rearrange("(i p) c -> p i c", p=P),
             )
-            return sb
+            return rows_sb
+
+        loaded = {}
 
         def load_batch(b):
-            return {
-                "x": load_rows("x_sb", x[b]),
-                "k_re": load_rows("k_re_sb", k_rot_re[b].rearrange("l h d -> l (h d)")),
-                "k_im": load_rows("k_im_sb", k_rot_im[b].rearrange("l h d -> l (h d)")),
-                "q_re": load_rows("q_re_sb", q_rot_re[b].rearrange("l h d -> l (h d)")),
-                "q_im": load_rows("q_im_sb", q_rot_im[b].rearrange("l h d -> l (h d)")),
+            loaded[b] = {
+                "k_re": load_rows(inputs, "k_re_sb", k_rot_re[b].rearrange("l h d -> l (h d)")),
+                "k_im": load_rows(inputs, "k_im_sb", k_rot_im[b].rearrange("l h d -> l (h d)")),
+                "q_re": load_rows(inputs, "q_re_sb", q_rot_re[b].rearrange("l h d -> l (h d)")),
+                "q_im": load_rows(inputs, "q_im_sb", q_rot_im[b].rearrange("l h d -> l (h d)")),
+                "x": load_rows(inputs, "x_sb", x[b]),
             }
 
-        w_sb = const.tile([P, TILES * DIM], BF16)
-        nc.sync.dma_start(
-            out=w_sb[:].rearrange("p (i c) -> p i c", i=TILES),
-            in_=wv_w.rearrange("(i p) c -> p i c", p=P),
-        )
-        loaded = {0: load_batch(0), 1: load_batch(1)}
         amp_logit = const.tile([P, H], BF16)
         nc.scalar.dma_start(out=amp_logit[:], in_=amplitude.partition_broadcast(P))
         bias = const.tile([P, DIM], BF16)
         nc.scalar.dma_start(out=bias[:], in_=wv_b.partition_broadcast(P))
+        load_batch(0)
+        w_sb = load_rows(const, "w_sb", wv_w)
+        load_batch(1)
 
         ident_bf16 = const.tile([P, P], BF16)
         make_identity(nc, ident_bf16[:])
         ident_f32 = const.tile([P, P], F32)
         make_identity(nc, ident_f32[:])
-
-        p_grouped = [
-            const.tile([P, TILES, P, PACK], BF16, name="p_grouped%d" % r, align_bytes=64)
-            for r in range(P_RING)
-        ]
-        for r in range(P_RING):
-            nc.vector.memset(p_grouped[r][:], 0.0)
+        minus_ident = const.tile([P, P], BF16)
+        nc.vector.tensor_scalar_mul(out=minus_ident[:], in0=ident_bf16[:], scalar1=-1.0)
 
         distance_i32 = const.tile([P, P, PACK], I32)
         nc.gpsimd.iota(
@@ -93,155 +88,183 @@ def tile_retention_pb_t_kernel(
                 out=decay_h[:], in0=distance[:], scalar1=log_amp[:, h : h + 1]
             )
             nc.scalar.activation(out=decay_h[:], in_=decay_h[:], func=ACT.Exp)
-            nc.vector.tensor_mul(out=decay_h[:], in0=decay_h[:], in1=causal[:])
             decay.append(decay_h)
+        for h in range(H):
+            nc.vector.tensor_mul(out=decay[h][:], in0=decay[h][:], in1=causal[:])
 
-        def quantise_channels_last(rows_sb, name):
+        p_grouped = [
+            const.tile([P, TILES, P, PACK], BF16, name="p_grouped%d" % r, align_bytes=64)
+            for r in range(P_RING)
+        ]
+        for r in range(P_RING):
+            nc.vector.memset(p_grouped[r][:].rearrange("p i j t -> p (i j t)").bitcast(I32), 0)
+
+        def flip_channels_last(rows_sb, name):
             words = rows_sb[:].bitcast(F32)
             grouped = work.tile([P, L * PACK], BF16, name=name + "_grouped", align_bytes=64)
             grouped_words = grouped[:].bitcast(F32).rearrange("p (r u) -> p r u", u=2)
             for half in range(2):
-                flipped = psum.tile([P, 2, 2 * P], F32, name="flipped_words")
+                bank = psum.tile([P, 2, 2 * P], F32, name="shared_bank", bufs=3)
                 for i in range(2):
                     for u in range(2):
                         first = (2 * half + i) * 2 * P + u * P
                         nc.tensor.transpose(
-                            flipped[:, u, i * P : (i + 1) * P],
+                            bank[:, u, i * P : (i + 1) * P],
                             words[:, first : first + P],
                             ident_f32[:],
                         )
                 nc.scalar.copy(
                     out=grouped_words[:, half * 2 * P : (half + 1) * 2 * P, :],
-                    in_=flipped[:].rearrange("p u r -> p r u"),
+                    in_=bank[:].rearrange("p u r -> p r u"),
                 )
-            codes = work.tile([P, L], U32, name=name + "_codes", align_bytes=64)
-            scales = work.tile([P, L], U8, name=name + "_scales", align_bytes=64)
-            nc.vector.quantize_mx(out=codes[:].bitcast(FP8X4), scales=scales[:], in_=grouped[:])
+            return grouped
+
+        def quantise(grouped_flat, name, bufs):
+            columns = grouped_flat.shape[1] // PACK
+            codes = work.tile([P, columns], U32, name=name + "_codes", bufs=bufs, align_bytes=64)
+            scales = work.tile([P, columns], U8, name=name + "_scales", bufs=bufs, align_bytes=64)
+            nc.vector.quantize_mx(out=codes[:].bitcast(FP8X4), scales=scales[:], in_=grouped_flat)
             return codes, scales
 
-        w_codes, w_scales = quantise_channels_last(w_sb, "w")
+        x_grouped = {}
+        x_quantised = {}
+        v_grouped = {}
+        v_quantised = {}
 
-        def project_values(x_codes, x_scales):
-            v_grouped = work.tile([P, H, D, PACK], BF16, align_bytes=64)
-            for h in range(H):
-                v_acc = psum.tile([P, TILES, D], F32)
-                for t in range(TILES):
-                    nc.tensor.matmul_mx(
-                        out=v_acc[:, t, :],
-                        lhsT=x_codes[:, t * P : (t + 1) * P].bitcast(FP8X4),
-                        lhsT_scale=x_scales[:, t * P : (t + 1) * P],
-                        rhs=w_codes[:, h * D : (h + 1) * D].bitcast(FP8X4),
-                        rhs_scale=w_scales[:, h * D : (h + 1) * D],
-                        start=True,
-                        stop=True,
-                    )
-                nc.vector.tensor_tensor(
-                    out=v_grouped[:, h, :, :],
-                    in0=v_acc[:].rearrange("p t d -> p d t"),
-                    in1=bias[:, h * D : (h + 1) * D].unsqueeze(2).to_broadcast([P, D, PACK]),
-                    op=ALU.add,
+        def project_values(unit):
+            b, h = divmod(unit, H)
+            x_codes, x_scales = x_quantised[b]
+            v_acc = psum.tile([P, TILES, D], F32, name="shared_bank", bufs=3)
+            for t in range(TILES):
+                nc.tensor.matmul_mx(
+                    out=v_acc[:, t, :],
+                    lhsT=x_codes[:, t * P : (t + 1) * P].bitcast(FP8X4),
+                    lhsT_scale=x_scales[:, t * P : (t + 1) * P],
+                    rhs=w_codes[:, h * D : (h + 1) * D].bitcast(FP8X4),
+                    rhs_scale=w_scales[:, h * D : (h + 1) * D],
+                    start=True,
+                    stop=True,
                 )
-            v_codes = work.tile([P, DIM], U32, align_bytes=64)
-            v_scales = work.tile([P, DIM], U8, align_bytes=64)
-            nc.vector.quantize_mx(
-                out=v_codes[:].bitcast(FP8X4),
-                scales=v_scales[:],
-                in_=v_grouped[:].rearrange("p h d t -> p (h d t)"),
+            v_grouped[unit] = work.tile([P, D, PACK], BF16, name="v_grouped", align_bytes=64)
+            nc.vector.tensor_tensor(
+                out=v_grouped[unit][:],
+                in0=v_acc[:].rearrange("p t d -> p d t"),
+                in1=bias[:, h * D : (h + 1) * D].unsqueeze(2).to_broadcast([P, D, PACK]),
+                op=ALU.add,
             )
-            return v_codes, v_scales
 
-        def flip_head(batch_sb, h):
-            flipped = {}
+        def quantise_values(unit):
+            v_quantised[unit] = quantise(
+                v_grouped[unit][:].rearrange("p d t -> p (d t)"), "v", 2 * H
+            )
+
+        flipped = {}
+
+        def flip_head(unit):
+            b, h = divmod(unit, H)
+            flipped[unit] = {}
             for who in ("q", "k"):
-                bank = psum.tile([P, 2, L], BF16, name="flipped_qk", bufs=2)
+                bank = psum.tile([P, 2 * L], BF16, name="flipped_bank", bufs=2)
                 for c, part in enumerate(("re", "im")):
-                    rows_sb = batch_sb[who + "_" + part]
+                    rows_sb = loaded[b][who + "_" + part]
                     for i in range(TILES):
-                        first = i * DIM + h * D
-                        nc.tensor.transpose(
-                            bank[:, c, i * P : (i + 1) * P],
-                            rows_sb[:, first : first + D],
-                            ident_bf16[:],
-                        )
-                flipped[who] = bank
-            q_t = work.tile([P, 2, L], BF16)
-            nc.scalar.copy(out=q_t[:], in_=flipped["q"][:])
-            k_t = work.tile([P, 2, L], BF16)
-            nc.scalar.copy(out=k_t[:, 0, :], in_=flipped["k"][:, 0, :])
-            nc.scalar.mul(out=k_t[:, 1, :], in_=flipped["k"][:, 1, :], mul=-1.0)
-            return q_t, k_t
+                        block = rows_sb[:, i * DIM + h * D : i * DIM + (h + 1) * D]
+                        place = bank[:, c * L + i * P : c * L + (i + 1) * P]
+                        if who == "k" and part == "im":
+                            nc.tensor.matmul(
+                                out=place, lhsT=block, rhs=minus_ident[:], start=True, stop=True
+                            )
+                        else:
+                            nc.tensor.transpose(place, block, ident_bf16[:])
+                flipped_sb = work.tile([P, 2 * L], BF16, name=who + "_flipped")
+                nc.scalar.copy(out=flipped_sb[:].bitcast(F32), in_=bank[:].bitcast(F32))
+                flipped[unit][who] = flipped_sb
 
-        def decayed_scores(unit, q_t, k_t):
+        def score_tile(unit, i):
             h = unit % H
+            q_flipped = flipped[unit]["q"]
+            k_flipped = flipped[unit]["k"]
             grouped = p_grouped[unit % P_RING]
-            for i in range(TILES):
-                keys = i + 1
-                scores = psum.tile([P, TILES, P], F32, bufs=3)
-                for t in range(keys):
-                    for c in range(2):
-                        nc.tensor.matmul(
-                            out=scores[:, t, :],
-                            lhsT=k_t[:, c, t * P : (t + 1) * P],
-                            rhs=q_t[:, c, i * P : (i + 1) * P],
-                            start=(c == 0),
-                            stop=(c == 1),
-                        )
+            keys = i + 1
+            scores = psum.tile([P, TILES, P], F32, bufs=3)
+            for t in range(keys):
+                for c in range(2):
+                    nc.tensor.matmul(
+                        out=scores[:, t, :],
+                        lhsT=k_flipped[:, c * L + t * P : c * L + (t + 1) * P],
+                        rhs=q_flipped[:, c * L + i * P : c * L + (i + 1) * P],
+                        start=(c == 0),
+                        stop=(c == 1),
+                    )
+            if i == 0:
+                dense = work.tile([P, P], BF16)
+                nc.vector.tensor_tensor(
+                    out=dense[:], in0=scores[:, 0, :], in1=decay[h][:, :, PACK - 1], op=ALU.mult
+                )
+                nc.scalar.copy(out=grouped[:, 0, :, 0], in_=dense[:])
+            else:
                 nc.vector.tensor_tensor(
                     out=grouped[:, i, :, 0:keys],
                     in0=scores[:, 0:keys, :].rearrange("p t j -> p j t"),
                     in1=decay[h][:, :, PACK - keys : PACK],
                     op=ALU.mult,
                 )
-            p_codes = work.tile([P, L], U32, align_bytes=64)
-            p_scales = work.tile([P, L], U8, align_bytes=64)
-            nc.vector.quantize_mx(
-                out=p_codes[:].bitcast(FP8X4),
-                scales=p_scales[:],
-                in_=grouped[:].rearrange("p i j t -> p (i j t)"),
-            )
-            return p_codes, p_scales
 
-        def weighted_values(h, p_codes, p_scales, v_codes, v_scales, out_sb):
-            o_acc = psum.tile([P, TILES, D], F32)
+        p_quantised = {}
+
+        def quantise_p(unit):
+            p_quantised[unit] = quantise(
+                p_grouped[unit % P_RING][:].rearrange("p i j t -> p (i j t)"), "p", 2
+            )
+
+        def weighted_values(unit):
+            b, h = divmod(unit, H)
+            p_codes, p_scales = p_quantised[unit]
+            v_codes, v_scales = v_quantised[unit]
+            o_acc = psum.tile([P, TILES, D], F32, name="shared_bank", bufs=3)
             for i in range(TILES):
                 nc.tensor.matmul_mx(
                     out=o_acc[:, i, :],
                     lhsT=p_codes[:, i * P : (i + 1) * P].bitcast(FP8X4),
                     lhsT_scale=p_scales[:, i * P : (i + 1) * P],
-                    rhs=v_codes[:, h * D : (h + 1) * D].bitcast(FP8X4),
-                    rhs_scale=v_scales[:, h * D : (h + 1) * D],
+                    rhs=v_codes[:].bitcast(FP8X4),
+                    rhs_scale=v_scales[:],
                     start=True,
                     stop=True,
                 )
-            nc.scalar.copy(out=out_sb[:, :, h * D : (h + 1) * D], in_=o_acc[:])
+            out_sb = work.tile([P, TILES, D], F32, bufs=3)
+            nc.scalar.copy(out=out_sb[:], in_=o_acc[:])
+            nc.sync.dma_start(
+                out=out[b].rearrange("(i p) c -> p i c", p=P)[:, :, h * D : (h + 1) * D],
+                in_=out_sb[:],
+            )
 
-        values = {0: project_values(*quantise_channels_last(loaded[0]["x"], "x"))}
-        heads = {0: flip_head(loaded[0], 0)}
-        x_quantised = {}
-        probs = {}
-        out_tiles = {}
-
-        def finish(unit):
-            b, h = divmod(unit, H)
-            if h == 0:
-                out_tiles[b] = work.tile([P, TILES, DIM], F32, name="out_sb")
-            weighted_values(h, *probs[unit], *values[b], out_tiles[b])
-            if h == H - 1:
-                nc.sync.dma_start(
-                    out=out[b].rearrange("(i p) c -> p i c", p=P), in_=out_tiles[b][:]
-                )
+        flip_head(0)
+        w_codes, w_scales = quantise(flip_channels_last(w_sb, "w")[:], "w", 1)
+        for b in range(2):
+            x_quantised[b] = quantise(flip_channels_last(loaded[b]["x"], "x")[:], "x", 2)
+        for unit in range(H):
+            project_values(unit)
+            quantise_values(unit)
 
         for unit in range(UNITS):
             b, h = divmod(unit, H)
             if h == 0 and b + 2 < B:
-                loaded[b + 2] = load_batch(b + 2)
+                load_batch(b + 2)
             if unit + 1 < UNITS:
-                heads[unit + 1] = flip_head(loaded[(unit + 1) // H], (unit + 1) % H)
-            if h == 1 and b + 1 < B:
-                x_quantised[b + 1] = quantise_channels_last(loaded[b + 1]["x"], "x")
-            probs[unit] = decayed_scores(unit, *heads[unit])
-            if h == 2 and b + 1 < B:
-                values[b + 1] = project_values(*x_quantised[b + 1])
-            if unit >= 1:
-                finish(unit - 1)
-        finish(UNITS - 1)
+                flip_head(unit + 1)
+            if h == H - 1 and b + 2 < B:
+                x_grouped[b + 2] = flip_channels_last(loaded[b + 2]["x"], "x")
+            for i in range(TILES):
+                if i == TILES - 1:
+                    if unit >= 1:
+                        weighted_values(unit - 1)
+                    if unit + H < UNITS:
+                        project_values(unit + H)
+                score_tile(unit, i)
+            if unit + H < UNITS:
+                quantise_values(unit + H)
+            quantise_p(unit)
+            if h == H - 1 and b + 2 < B:
+                x_quantised[b + 2] = quantise(x_grouped[b + 2][:], "x", 2)
+        weighted_values(UNITS - 1)

@@ -81,16 +81,21 @@ def tile_retention_pb_t_kernel(
         nc.scalar.activation(out=amp[:], in_=amp_logit[:], func=ACT.Sigmoid)
         log_amp = const.tile([P, H], F32)
         nc.scalar.activation(out=log_amp[:], in_=amp[:], func=ACT.Ln)
-        decay = []
-        for h in range(H):
-            decay_h = const.tile([P, P, PACK], F32, name="decay%d" % h)
+        decay = {}
+        decay_first = {}
+
+        def build_decay(h):
+            decay[h] = const.tile([P, P, PACK], F32, name="decay%d" % h)
             nc.vector.tensor_scalar_mul(
-                out=decay_h[:], in0=distance[:], scalar1=log_amp[:, h : h + 1]
+                out=decay[h][:], in0=distance[:], scalar1=log_amp[:, h : h + 1]
             )
-            nc.scalar.activation(out=decay_h[:], in_=decay_h[:], func=ACT.Exp)
-            decay.append(decay_h)
-        for h in range(H):
+            nc.scalar.activation(out=decay[h][:], in_=decay[h][:], func=ACT.Exp)
             nc.vector.tensor_mul(out=decay[h][:], in0=decay[h][:], in1=causal[:])
+            decay_first[h] = const.tile([P, P, 3], F32, name="decay_first%d" % h)
+            nc.vector.tensor_copy(out=decay_first[h][:, :, 0], in_=decay[h][:, :, 3])
+            nc.vector.tensor_copy(out=decay_first[h][:, :, 1:3], in_=decay[h][:, :, 2:4])
+
+        build_decay(0)
 
         p_grouped = [
             const.tile([P, TILES, P, PACK], BF16, name="p_grouped%d" % r, align_bytes=64)
@@ -128,6 +133,7 @@ def tile_retention_pb_t_kernel(
 
         x_grouped = {}
         x_quantised = {}
+        v_sums = {}
         v_grouped = {}
         v_quantised = {}
 
@@ -145,17 +151,21 @@ def tile_retention_pb_t_kernel(
                     start=True,
                     stop=True,
                 )
+            v_sums[unit] = v_acc
+
+        def add_bias(unit):
+            h = unit % H
             v_grouped[unit] = work.tile([P, D, PACK], BF16, name="v_grouped", align_bytes=64)
             nc.vector.tensor_tensor(
                 out=v_grouped[unit][:],
-                in0=v_acc[:].rearrange("p t d -> p d t"),
+                in0=v_sums[unit][:].rearrange("p t d -> p d t"),
                 in1=bias[:, h * D : (h + 1) * D].unsqueeze(2).to_broadcast([P, D, PACK]),
                 op=ALU.add,
             )
 
         def quantise_values(unit):
             v_quantised[unit] = quantise(
-                v_grouped[unit][:].rearrange("p d t -> p (d t)"), "v", 2 * H
+                v_grouped[unit][:].rearrange("p d t -> p (d t)"), "v", 3
             )
 
         flipped = {}
@@ -163,7 +173,7 @@ def tile_retention_pb_t_kernel(
         def flip_head(unit):
             b, h = divmod(unit, H)
             flipped[unit] = {}
-            for who in ("q", "k"):
+            for who in ("k", "q"):
                 bank = psum.tile([P, 2 * L], BF16, name="flipped_bank", bufs=2)
                 for c, part in enumerate(("re", "im")):
                     rows_sb = loaded[b][who + "_" + part]
@@ -180,41 +190,55 @@ def tile_retention_pb_t_kernel(
                 nc.scalar.copy(out=flipped_sb[:].bitcast(F32), in_=bank[:].bitcast(F32))
                 flipped[unit][who] = flipped_sb
 
-        def score_tile(unit, i):
-            h = unit % H
+        def score_matmuls(unit, i, t, place):
             q_flipped = flipped[unit]["q"]
             k_flipped = flipped[unit]["k"]
+            for c in range(2):
+                nc.tensor.matmul(
+                    out=place,
+                    lhsT=k_flipped[:, c * L + t * P : c * L + (t + 1) * P],
+                    rhs=q_flipped[:, c * L + i * P : c * L + (i + 1) * P],
+                    start=(c == 0),
+                    stop=(c == 1),
+                )
+
+        dense_first = {}
+
+        def first_query_tiles(unit):
+            scores = psum.tile([P, TILES, P], F32, bufs=3)
+            score_matmuls(unit, 0, 0, scores[:, 0, :])
+            score_matmuls(unit, 1, 0, scores[:, 1, :])
+            score_matmuls(unit, 1, 1, scores[:, 2, :])
+            dense_first[unit] = work.tile([P, P, 3], BF16, name="dense_first")
+            nc.vector.tensor_tensor(
+                out=dense_first[unit][:],
+                in0=scores[:, 0:3, :].rearrange("p s j -> p j s"),
+                in1=decay_first[unit % H][:],
+                op=ALU.mult,
+            )
+
+        def spread_first_query_tiles(unit):
             grouped = p_grouped[unit % P_RING]
+            nc.scalar.copy(out=grouped[:, 0, :, 0], in_=dense_first[unit][:, :, 0])
+            nc.scalar.copy(out=grouped[:, 1, :, 0:2], in_=dense_first[unit][:, :, 1:3])
+
+        def query_tile(unit, i):
             keys = i + 1
             scores = psum.tile([P, TILES, P], F32, bufs=3)
             for t in range(keys):
-                for c in range(2):
-                    nc.tensor.matmul(
-                        out=scores[:, t, :],
-                        lhsT=k_flipped[:, c * L + t * P : c * L + (t + 1) * P],
-                        rhs=q_flipped[:, c * L + i * P : c * L + (i + 1) * P],
-                        start=(c == 0),
-                        stop=(c == 1),
-                    )
-            if i == 0:
-                dense = work.tile([P, P], BF16)
-                nc.vector.tensor_tensor(
-                    out=dense[:], in0=scores[:, 0, :], in1=decay[h][:, :, PACK - 1], op=ALU.mult
-                )
-                nc.scalar.copy(out=grouped[:, 0, :, 0], in_=dense[:])
-            else:
-                nc.vector.tensor_tensor(
-                    out=grouped[:, i, :, 0:keys],
-                    in0=scores[:, 0:keys, :].rearrange("p t j -> p j t"),
-                    in1=decay[h][:, :, PACK - keys : PACK],
-                    op=ALU.mult,
-                )
+                score_matmuls(unit, i, t, scores[:, t, :])
+            nc.vector.tensor_tensor(
+                out=p_grouped[unit % P_RING][:, i, :, 0:keys],
+                in0=scores[:, 0:keys, :].rearrange("p t j -> p j t"),
+                in1=decay[unit % H][:, :, PACK - keys : PACK],
+                op=ALU.mult,
+            )
 
         p_quantised = {}
 
         def quantise_p(unit):
             p_quantised[unit] = quantise(
-                p_grouped[unit % P_RING][:].rearrange("p i j t -> p (i j t)"), "p", 2
+                p_grouped[unit % P_RING][:].rearrange("p i j t -> p (i j t)"), "p", 3
             )
 
         def weighted_values(unit):
@@ -240,31 +264,39 @@ def tile_retention_pb_t_kernel(
             )
 
         flip_head(0)
-        w_codes, w_scales = quantise(flip_channels_last(w_sb, "w")[:], "w", 1)
-        for b in range(2):
-            x_quantised[b] = quantise(flip_channels_last(loaded[b]["x"], "x")[:], "x", 2)
-        for unit in range(H):
-            project_values(unit)
-            quantise_values(unit)
-
         for unit in range(UNITS):
             b, h = divmod(unit, H)
             if h == 0 and b + 2 < B:
                 load_batch(b + 2)
             if unit + 1 < UNITS:
                 flip_head(unit + 1)
-            if h == H - 1 and b + 2 < B:
-                x_grouped[b + 2] = flip_channels_last(loaded[b + 2]["x"], "x")
-            for i in range(TILES):
-                if i == TILES - 1:
-                    if unit >= 1:
-                        weighted_values(unit - 1)
-                    if unit + H < UNITS:
-                        project_values(unit + H)
-                score_tile(unit, i)
-            if unit + H < UNITS:
-                quantise_values(unit + H)
+            first_query_tiles(unit)
+            if unit == 0:
+                w_grouped = flip_channels_last(w_sb, "w")
+                x_grouped[0] = flip_channels_last(loaded[0]["x"], "x")
+            if h == H - 1 and b + 1 < B:
+                x_grouped[b + 1] = flip_channels_last(loaded[b + 1]["x"], "x")
+            query_tile(unit, 2)
+            if unit >= 2:
+                weighted_values(unit - 2)
+            if unit >= 1:
+                project_values(unit - 1)
+            spread_first_query_tiles(unit)
+            query_tile(unit, 3)
+            if unit >= 1:
+                add_bias(unit - 1)
             quantise_p(unit)
-            if h == H - 1 and b + 2 < B:
-                x_quantised[b + 2] = quantise(x_grouped[b + 2][:], "x", 2)
+            if unit >= 1:
+                quantise_values(unit - 1)
+            if unit == 0:
+                w_codes, w_scales = quantise(w_grouped[:], "w", 1)
+                x_quantised[0] = quantise(x_grouped[0][:], "x", 2)
+            if h == H - 1 and b + 1 < B:
+                x_quantised[b + 1] = quantise(x_grouped[b + 1][:], "x", 2)
+            if unit + 1 < H:
+                build_decay(unit + 1)
+        project_values(UNITS - 1)
+        add_bias(UNITS - 1)
+        quantise_values(UNITS - 1)
+        weighted_values(UNITS - 2)
         weighted_values(UNITS - 1)

@@ -19,6 +19,8 @@ PACK = 4
 TILES = L // P
 UNITS = B * H
 P_RING = 3
+OUT_LAG = 3
+FLIP_AHEAD = 2
 
 FLOPS = 2 * B * L * DIM * DIM + 3 * 2 * B * H * L * L * D
 
@@ -46,10 +48,10 @@ def tile_retention_pb_t_kernel(
 
         def load_batch(b):
             loaded[b] = {
-                "k_re": load_rows(inputs, "k_re_sb", k_rot_re[b].rearrange("l h d -> l (h d)")),
-                "k_im": load_rows(inputs, "k_im_sb", k_rot_im[b].rearrange("l h d -> l (h d)")),
                 "q_re": load_rows(inputs, "q_re_sb", q_rot_re[b].rearrange("l h d -> l (h d)")),
                 "q_im": load_rows(inputs, "q_im_sb", q_rot_im[b].rearrange("l h d -> l (h d)")),
+                "k_re": load_rows(inputs, "k_re_sb", k_rot_re[b].rearrange("l h d -> l (h d)")),
+                "k_im": load_rows(inputs, "k_im_sb", k_rot_im[b].rearrange("l h d -> l (h d)")),
                 "x": load_rows(inputs, "x_sb", x[b]),
             }
 
@@ -165,50 +167,64 @@ def tile_retention_pb_t_kernel(
 
         def quantise_values(unit):
             v_quantised[unit] = quantise(
-                v_grouped[unit][:].rearrange("p d t -> p (d t)"), "v", 3
+                v_grouped[unit][:].rearrange("p d t -> p (d t)"), "v", OUT_LAG
             )
 
         flipped = {}
 
-        def flip_head(unit):
+        def flip_block(bank, unit, who, n):
             b, h = divmod(unit, H)
-            flipped[unit] = {}
-            for who in ("k", "q"):
-                bank = psum.tile([P, 2 * L], BF16, name="flipped_bank", bufs=2)
-                for c, part in enumerate(("re", "im")):
-                    rows_sb = loaded[b][who + "_" + part]
-                    for i in range(TILES):
-                        block = rows_sb[:, i * DIM + h * D : i * DIM + (h + 1) * D]
-                        place = bank[:, c * L + i * P : c * L + (i + 1) * P]
-                        if who == "k" and part == "im":
-                            nc.tensor.matmul(
-                                out=place, lhsT=block, rhs=minus_ident[:], start=True, stop=True
-                            )
-                        else:
-                            nc.tensor.transpose(place, block, ident_bf16[:])
-                flipped_sb = work.tile([P, 2 * L], BF16, name=who + "_flipped")
-                nc.scalar.copy(out=flipped_sb[:].bitcast(F32), in_=bank[:].bitcast(F32))
-                flipped[unit][who] = flipped_sb
+            c, i = divmod(n, TILES)
+            rows_sb = loaded[b][who + ("_re", "_im")[c]]
+            block = rows_sb[:, i * DIM + h * D : i * DIM + (h + 1) * D]
+            place = bank[:, n * P : (n + 1) * P]
+            if who == "k" and c == 1:
+                nc.tensor.matmul(out=place, lhsT=block, rhs=minus_ident[:], start=True, stop=True)
+            else:
+                nc.tensor.transpose(place, block, ident_bf16[:])
 
-        def score_matmuls(unit, i, t, place):
-            q_flipped = flipped[unit]["q"]
-            k_flipped = flipped[unit]["k"]
-            for c in range(2):
-                nc.tensor.matmul(
-                    out=place,
-                    lhsT=k_flipped[:, c * L + t * P : c * L + (t + 1) * P],
-                    rhs=q_flipped[:, c * L + i * P : c * L + (i + 1) * P],
-                    start=(c == 0),
-                    stop=(c == 1),
-                )
+        def score_matmul(unit, i, t, c, place):
+            nc.tensor.matmul(
+                out=place,
+                lhsT=flipped[unit]["k"][:, c * L + t * P : c * L + (t + 1) * P],
+                rhs=flipped[unit]["q"][:, c * L + i * P : c * L + (i + 1) * P],
+                start=(c == 0),
+                stop=(c == 1),
+            )
+
+        def scores_and_flips(unit, tiles, who):
+            later = unit + FLIP_AHEAD
+            scores = psum.tile([P, TILES, P], F32, bufs=3)
+            matmuls = [(i, t, c, place) for place, (i, t) in enumerate(tiles) for c in range(2)]
+            if who is not None and later < UNITS:
+                bank = psum.tile([P, 2 * L], BF16, name="flipped_bank", bufs=2)
+                for n in range(2 * TILES):
+                    flip_block(bank, later, who, n)
+                    if n < len(matmuls):
+                        i, t, c, place = matmuls[n]
+                        score_matmul(unit, i, t, c, scores[:, place, :])
+                copy_flipped(bank, later, who)
+            else:
+                for i, t, c, place in matmuls:
+                    score_matmul(unit, i, t, c, scores[:, place, :])
+            return scores
+
+        def copy_flipped(bank, unit, who):
+            flipped_sb = work.tile([P, 2 * L], BF16, name=who + "_flipped", bufs=FLIP_AHEAD + 1)
+            nc.scalar.copy(out=flipped_sb[:].bitcast(F32), in_=bank[:].bitcast(F32))
+            flipped[unit][who] = flipped_sb
+
+        def flip_head(unit):
+            for who in ("q", "k"):
+                bank = psum.tile([P, 2 * L], BF16, name="flipped_bank", bufs=2)
+                for n in range(2 * TILES):
+                    flip_block(bank, unit, who, n)
+                copy_flipped(bank, unit, who)
 
         dense_first = {}
 
         def first_query_tiles(unit):
-            scores = psum.tile([P, TILES, P], F32, bufs=3)
-            score_matmuls(unit, 0, 0, scores[:, 0, :])
-            score_matmuls(unit, 1, 0, scores[:, 1, :])
-            score_matmuls(unit, 1, 1, scores[:, 2, :])
+            scores = scores_and_flips(unit, [(0, 0), (1, 0), (1, 1)], "q")
             dense_first[unit] = work.tile([P, P, 3], BF16, name="dense_first")
             nc.vector.tensor_tensor(
                 out=dense_first[unit][:],
@@ -222,11 +238,9 @@ def tile_retention_pb_t_kernel(
             nc.scalar.copy(out=grouped[:, 0, :, 0], in_=dense_first[unit][:, :, 0])
             nc.scalar.copy(out=grouped[:, 1, :, 0:2], in_=dense_first[unit][:, :, 1:3])
 
-        def query_tile(unit, i):
+        def query_tile(unit, i, who):
             keys = i + 1
-            scores = psum.tile([P, TILES, P], F32, bufs=3)
-            for t in range(keys):
-                score_matmuls(unit, i, t, scores[:, t, :])
+            scores = scores_and_flips(unit, [(i, t) for t in range(keys)], who)
             nc.vector.tensor_tensor(
                 out=p_grouped[unit % P_RING][:, i, :, 0:keys],
                 in0=scores[:, 0:keys, :].rearrange("p t j -> p j t"),
@@ -238,7 +252,7 @@ def tile_retention_pb_t_kernel(
 
         def quantise_p(unit):
             p_quantised[unit] = quantise(
-                p_grouped[unit % P_RING][:].rearrange("p i j t -> p (i j t)"), "p", 3
+                p_grouped[unit % P_RING][:].rearrange("p i j t -> p (i j t)"), "p", OUT_LAG + 1
             )
 
         def weighted_values(unit):
@@ -263,26 +277,27 @@ def tile_retention_pb_t_kernel(
                 in_=out_sb[:],
             )
 
-        flip_head(0)
+        for unit in range(UNITS):
+            flipped[unit] = {}
+        for unit in range(FLIP_AHEAD):
+            flip_head(unit)
         for unit in range(UNITS):
             b, h = divmod(unit, H)
             if h == 0 and b + 2 < B:
                 load_batch(b + 2)
-            if unit + 1 < UNITS:
-                flip_head(unit + 1)
+            if h == H - 1 and b + 1 < B:
+                x_grouped[b + 1] = flip_channels_last(loaded[b + 1]["x"], "x")
             first_query_tiles(unit)
             if unit == 0:
                 w_grouped = flip_channels_last(w_sb, "w")
                 x_grouped[0] = flip_channels_last(loaded[0]["x"], "x")
-            if h == H - 1 and b + 1 < B:
-                x_grouped[b + 1] = flip_channels_last(loaded[b + 1]["x"], "x")
-            query_tile(unit, 2)
-            if unit >= 2:
-                weighted_values(unit - 2)
+            query_tile(unit, 2, "k")
+            if unit >= OUT_LAG:
+                weighted_values(unit - OUT_LAG)
             if unit >= 1:
                 project_values(unit - 1)
             spread_first_query_tiles(unit)
-            query_tile(unit, 3)
+            query_tile(unit, 3, None)
             if unit >= 1:
                 add_bias(unit - 1)
             quantise_p(unit)
@@ -298,5 +313,5 @@ def tile_retention_pb_t_kernel(
         project_values(UNITS - 1)
         add_bias(UNITS - 1)
         quantise_values(UNITS - 1)
-        weighted_values(UNITS - 2)
-        weighted_values(UNITS - 1)
+        for unit in range(UNITS - OUT_LAG, UNITS):
+            weighted_values(unit)

@@ -135,7 +135,6 @@ def tile_retention_pb_t_kernel(
 
         x_grouped = {}
         x_quantised = {}
-        v_sums = {}
         v_grouped = {}
         v_quantised = {}
 
@@ -153,21 +152,19 @@ def tile_retention_pb_t_kernel(
                     start=True,
                     stop=True,
                 )
-            v_sums[unit] = v_acc
-
-        def add_bias(unit):
-            h = unit % H
-            v_grouped[unit] = work.tile([P, D, PACK], BF16, name="v_grouped", align_bytes=64)
-            nc.vector.tensor_tensor(
+            v_sums = work.tile([P, D, PACK], F32, bufs=3)
+            nc.scalar.copy(out=v_sums[:], in_=v_acc[:].rearrange("p t d -> p d t"))
+            v_grouped[unit] = work.tile([P, D, PACK], BF16, name="v_grouped", bufs=4, align_bytes=64)
+            nc.gpsimd.tensor_tensor(
                 out=v_grouped[unit][:],
-                in0=v_sums[unit][:].rearrange("p t d -> p d t"),
+                in0=v_sums[:],
                 in1=bias[:, h * D : (h + 1) * D].unsqueeze(2).to_broadcast([P, D, PACK]),
                 op=ALU.add,
             )
 
         def quantise_values(unit):
             v_quantised[unit] = quantise(
-                v_grouped[unit][:].rearrange("p d t -> p (d t)"), "v", OUT_LAG
+                v_grouped[unit][:].rearrange("p d t -> p (d t)"), "v", OUT_LAG + 2
             )
 
         flipped = {}
@@ -236,7 +233,14 @@ def tile_retention_pb_t_kernel(
         def spread_first_query_tiles(unit):
             grouped = p_grouped[unit % P_RING]
             nc.scalar.copy(out=grouped[:, 0, :, 0], in_=dense_first[unit][:, :, 0])
-            nc.scalar.copy(out=grouped[:, 1, :, 0:2], in_=dense_first[unit][:, :, 1:3])
+            nc.gpsimd.tensor_scalar(
+                out=grouped[:, 1, :, 0:2],
+                in0=dense_first[unit][:, :, 1:3],
+                scalar1=1.0,
+                scalar2=0.0,
+                op0=ALU.mult,
+                op1=ALU.add,
+            )
 
         def query_tile(unit, i, who):
             keys = i + 1
@@ -285,33 +289,36 @@ def tile_retention_pb_t_kernel(
             b, h = divmod(unit, H)
             if h == 0 and b + 2 < B:
                 load_batch(b + 2)
-            if h == H - 1 and b + 1 < B:
+            if h == H - 2 and b + 1 < B:
                 x_grouped[b + 1] = flip_channels_last(loaded[b + 1]["x"], "x")
             first_query_tiles(unit)
             if unit == 0:
                 w_grouped = flip_channels_last(w_sb, "w")
                 x_grouped[0] = flip_channels_last(loaded[0]["x"], "x")
             query_tile(unit, 2, "k")
+            spread_first_query_tiles(unit)
             if unit >= OUT_LAG:
                 weighted_values(unit - OUT_LAG)
+            if unit == 1:
+                project_values(0)
+                project_values(1)
+            if 1 <= unit < UNITS - 1:
+                project_values(unit + 1)
             if unit >= 1:
-                project_values(unit - 1)
-            spread_first_query_tiles(unit)
-            query_tile(unit, 3, None)
-            if unit >= 1:
-                add_bias(unit - 1)
-            quantise_p(unit)
-            if unit >= 1:
-                quantise_values(unit - 1)
+                quantise_p(unit - 1)
+            if unit == 2:
+                quantise_values(0)
+                quantise_values(1)
+            if unit >= 2:
+                quantise_values(unit)
             if unit == 0:
                 w_codes, w_scales = quantise(w_grouped[:], "w", 1)
                 x_quantised[0] = quantise(x_grouped[0][:], "x", 2)
-            if h == H - 1 and b + 1 < B:
+            if h == H - 2 and b + 1 < B:
                 x_quantised[b + 1] = quantise(x_grouped[b + 1][:], "x", 2)
+            query_tile(unit, 3, None)
             if unit + 1 < H:
                 build_decay(unit + 1)
-        project_values(UNITS - 1)
-        add_bias(UNITS - 1)
-        quantise_values(UNITS - 1)
+        quantise_p(UNITS - 1)
         for unit in range(UNITS - OUT_LAG, UNITS):
             weighted_values(unit)

@@ -57,10 +57,10 @@ def tile_retention_pb_t_kernel(
 
         amp_logit = const.tile([P, H], BF16)
         nc.scalar.dma_start(out=amp_logit[:], in_=amplitude.partition_broadcast(P))
-        bias = const.tile([P, DIM], BF16)
-        nc.scalar.dma_start(out=bias[:], in_=wv_b.partition_broadcast(P))
         load_batch(0)
         w_sb = load_rows(const, "w_sb", wv_w)
+        bias = const.tile([P, DIM], BF16)
+        nc.sync.dma_start(out=bias[:], in_=wv_b.partition_broadcast(P))
         load_batch(1)
 
         ident_bf16 = const.tile([P, P], BF16)
@@ -84,7 +84,6 @@ def tile_retention_pb_t_kernel(
         log_amp = const.tile([P, H], F32)
         nc.scalar.activation(out=log_amp[:], in_=amp[:], func=ACT.Ln)
         decay = {}
-        decay_first = {}
 
         def build_decay(h):
             decay[h] = const.tile([P, P, PACK], F32, name="decay%d" % h)
@@ -93,9 +92,6 @@ def tile_retention_pb_t_kernel(
             )
             nc.scalar.activation(out=decay[h][:], in_=decay[h][:], func=ACT.Exp)
             nc.vector.tensor_mul(out=decay[h][:], in0=decay[h][:], in1=causal[:])
-            decay_first[h] = const.tile([P, P, 3], F32, name="decay_first%d" % h)
-            nc.vector.tensor_copy(out=decay_first[h][:, :, 0], in_=decay[h][:, :, 3])
-            nc.vector.tensor_copy(out=decay_first[h][:, :, 1:3], in_=decay[h][:, :, 2:4])
 
         build_decay(0)
 
@@ -218,39 +214,23 @@ def tile_retention_pb_t_kernel(
                     flip_block(bank, unit, who, n)
                 copy_flipped(bank, unit, who)
 
-        dense_first = {}
-
-        def first_query_tiles(unit):
-            scores = scores_and_flips(unit, [(0, 0), (1, 0), (1, 1)], "q")
-            dense_first[unit] = work.tile([P, P, 3], BF16, name="dense_first")
-            nc.vector.tensor_tensor(
-                out=dense_first[unit][:],
-                in0=scores[:, 0:3, :].rearrange("p s j -> p j s"),
-                in1=decay_first[unit % H][:],
-                op=ALU.mult,
-            )
-
-        def spread_first_query_tiles(unit):
-            grouped = p_grouped[unit % P_RING]
-            nc.scalar.copy(out=grouped[:, 0, :, 0], in_=dense_first[unit][:, :, 0])
-            nc.gpsimd.tensor_scalar(
-                out=grouped[:, 1, :, 0:2],
-                in0=dense_first[unit][:, :, 1:3],
-                scalar1=1.0,
-                scalar2=0.0,
-                op0=ALU.mult,
-                op1=ALU.add,
-            )
-
-        def query_tile(unit, i, who):
+        def multiply_by_decay(unit, scores, place, i):
             keys = i + 1
-            scores = scores_and_flips(unit, [(i, t) for t in range(keys)], who)
             nc.vector.tensor_tensor(
                 out=p_grouped[unit % P_RING][:, i, :, 0:keys],
-                in0=scores[:, 0:keys, :].rearrange("p t j -> p j t"),
+                in0=scores[:, place : place + keys, :].rearrange("p t j -> p j t"),
                 in1=decay[unit % H][:, :, PACK - keys : PACK],
                 op=ALU.mult,
             )
+
+        def first_query_tiles(unit):
+            scores = scores_and_flips(unit, [(0, 0), (1, 0), (1, 1)], "q")
+            multiply_by_decay(unit, scores, 0, 0)
+            multiply_by_decay(unit, scores, 1, 1)
+
+        def query_tile(unit, i, who):
+            scores = scores_and_flips(unit, [(i, t) for t in range(i + 1)], who)
+            multiply_by_decay(unit, scores, 0, i)
 
         p_quantised = {}
 
@@ -292,11 +272,7 @@ def tile_retention_pb_t_kernel(
             if h == H - 2 and b + 1 < B:
                 x_grouped[b + 1] = flip_channels_last(loaded[b + 1]["x"], "x")
             first_query_tiles(unit)
-            if unit == 0:
-                w_grouped = flip_channels_last(w_sb, "w")
-                x_grouped[0] = flip_channels_last(loaded[0]["x"], "x")
             query_tile(unit, 2, "k")
-            spread_first_query_tiles(unit)
             if unit >= OUT_LAG:
                 weighted_values(unit - OUT_LAG)
             if unit == 1:
@@ -311,12 +287,14 @@ def tile_retention_pb_t_kernel(
                 quantise_values(1)
             if unit >= 2:
                 quantise_values(unit)
-            if unit == 0:
-                w_codes, w_scales = quantise(w_grouped[:], "w", 1)
-                x_quantised[0] = quantise(x_grouped[0][:], "x", 2)
             if h == H - 2 and b + 1 < B:
                 x_quantised[b + 1] = quantise(x_grouped[b + 1][:], "x", 2)
             query_tile(unit, 3, None)
+            if unit == 0:
+                w_grouped = flip_channels_last(w_sb, "w")
+                x_grouped[0] = flip_channels_last(loaded[0]["x"], "x")
+                w_codes, w_scales = quantise(w_grouped[:], "w", 1)
+                x_quantised[0] = quantise(x_grouped[0][:], "x", 2)
             if unit + 1 < H:
                 build_decay(unit + 1)
         quantise_p(UNITS - 1)

@@ -20,6 +20,7 @@ TILES = L // P
 UNITS = B * H
 P_RING = 3
 OUT_LAG = 3
+END_LAG = 2
 FLIP_AHEAD = 2
 
 FLOPS = 2 * B * L * DIM * DIM + 3 * 2 * B * H * L * L * D
@@ -87,11 +88,12 @@ def tile_retention_pb_t_kernel(
 
         def build_decay(h):
             decay[h] = const.tile([P, P, PACK], F32, name="decay%d" % h)
-            nc.vector.tensor_scalar_mul(
-                out=decay[h][:], in0=distance[:], scalar1=log_amp[:, h : h + 1]
+            nc.scalar.activation(
+                out=decay[h][:], in_=distance[:], func=ACT.Exp, scale=log_amp[:, h : h + 1]
             )
-            nc.scalar.activation(out=decay[h][:], in_=decay[h][:], func=ACT.Exp)
-            nc.vector.tensor_mul(out=decay[h][:], in0=decay[h][:], in1=causal[:])
+            nc.gpsimd.tensor_tensor(
+                out=decay[h][:], in0=decay[h][:], in1=causal[:], op=ALU.mult
+            )
 
         build_decay(0)
 
@@ -207,12 +209,11 @@ def tile_retention_pb_t_kernel(
             nc.scalar.copy(out=flipped_sb[:].bitcast(F32), in_=bank[:].bitcast(F32))
             flipped[unit][who] = flipped_sb
 
-        def flip_head(unit):
-            for who in ("q", "k"):
-                bank = psum.tile([P, 2 * L], BF16, name="flipped_bank", bufs=2)
-                for n in range(2 * TILES):
-                    flip_block(bank, unit, who, n)
-                copy_flipped(bank, unit, who)
+        def flip_in_a_row(unit, who):
+            bank = psum.tile([P, 2 * L], BF16, name="flipped_bank", bufs=2)
+            for n in range(2 * TILES):
+                flip_block(bank, unit, who, n)
+            copy_flipped(bank, unit, who)
 
         def multiply_by_decay(unit, scores, place, i):
             keys = i + 1
@@ -234,37 +235,43 @@ def tile_retention_pb_t_kernel(
 
         p_quantised = {}
 
-        def quantise_p(unit):
-            p_quantised[unit] = quantise(
-                p_grouped[unit % P_RING][:].rearrange("p i j t -> p (i j t)"), "p", OUT_LAG + 1
-            )
+        def quantise_p(unit, first=0, count=TILES):
+            grouped = p_grouped[unit % P_RING][:, first : first + count, :, :]
+            name, bufs = ("p", OUT_LAG + 1) if count == TILES else ("p_from%d" % first, 1)
+            codes, scales = quantise(grouped.rearrange("p i j t -> p (i j t)"), name, bufs)
+            for n in range(count):
+                columns = slice(n * P, (n + 1) * P)
+                p_quantised[unit, first + n] = (codes[:, columns], scales[:, columns])
 
-        def weighted_values(unit):
+        def weighted_values(unit, first=0, count=TILES, copy=nc.scalar.copy):
             b, h = divmod(unit, H)
-            p_codes, p_scales = p_quantised[unit]
             v_codes, v_scales = v_quantised[unit]
             o_acc = psum.tile([P, TILES, D], F32, name="shared_bank", bufs=3)
-            for i in range(TILES):
+            for i in range(first, first + count):
+                p_codes, p_scales = p_quantised[unit, i]
                 nc.tensor.matmul_mx(
                     out=o_acc[:, i, :],
-                    lhsT=p_codes[:, i * P : (i + 1) * P].bitcast(FP8X4),
-                    lhsT_scale=p_scales[:, i * P : (i + 1) * P],
+                    lhsT=p_codes.bitcast(FP8X4),
+                    lhsT_scale=p_scales,
                     rhs=v_codes[:].bitcast(FP8X4),
                     rhs_scale=v_scales[:],
                     start=True,
                     stop=True,
                 )
+            tiles = slice(first, first + count)
             out_sb = work.tile([P, TILES, D], F32, bufs=3)
-            nc.scalar.copy(out=out_sb[:], in_=o_acc[:])
+            copy(out=out_sb[:, tiles, :], in_=o_acc[:, tiles, :])
             nc.sync.dma_start(
-                out=out[b].rearrange("(i p) c -> p i c", p=P)[:, :, h * D : (h + 1) * D],
-                in_=out_sb[:],
+                out=out[b].rearrange("(i p) c -> p i c", p=P)[:, tiles, h * D : (h + 1) * D],
+                in_=out_sb[:, tiles, :],
             )
 
         for unit in range(UNITS):
             flipped[unit] = {}
-        for unit in range(FLIP_AHEAD):
-            flip_head(unit)
+        for who in ("q", "k"):
+            for unit in range(FLIP_AHEAD):
+                flip_in_a_row(unit, who)
+        outs_done = 0
         for unit in range(UNITS):
             b, h = divmod(unit, H)
             if h == 0 and b + 2 < B:
@@ -273,8 +280,10 @@ def tile_retention_pb_t_kernel(
                 x_grouped[b + 1] = flip_channels_last(loaded[b + 1]["x"], "x")
             first_query_tiles(unit)
             query_tile(unit, 2, "k")
-            if unit >= OUT_LAG:
-                weighted_values(unit - OUT_LAG)
+            lag = OUT_LAG if unit + FLIP_AHEAD < UNITS else END_LAG
+            for ready in range(outs_done, unit - lag + 1):
+                weighted_values(ready)
+            outs_done = max(outs_done, unit - lag + 1)
             if unit == 1:
                 project_values(0)
                 project_values(1)
@@ -289,6 +298,9 @@ def tile_retention_pb_t_kernel(
                 quantise_values(unit)
             if h == H - 2 and b + 1 < B:
                 x_quantised[b + 1] = quantise(x_grouped[b + 1][:], "x", 2)
+            if unit == UNITS - 1:
+                quantise_p(unit, 0, 2)
+                quantise_p(unit, 2, 1)
             query_tile(unit, 3, None)
             if unit == 0:
                 w_grouped = flip_channels_last(w_sb, "w")
@@ -297,6 +309,9 @@ def tile_retention_pb_t_kernel(
                 x_quantised[0] = quantise(x_grouped[0][:], "x", 2)
             if unit + 1 < H:
                 build_decay(unit + 1)
-        quantise_p(UNITS - 1)
-        for unit in range(UNITS - OUT_LAG, UNITS):
+        last = UNITS - 1
+        quantise_p(last, 3, 1)
+        for unit in range(outs_done, last):
             weighted_values(unit)
+        weighted_values(last, 0, 3)
+        weighted_values(last, 3, 1, nc.vector.tensor_copy)

@@ -71,38 +71,37 @@ def tile_retention_pb_t_kernel(
         minus_ident = const.tile([P, P], BF16)
         nc.vector.tensor_scalar_mul(out=minus_ident[:], in0=ident_bf16[:], scalar1=-1.0)
 
-        distance_i32 = const.tile([P, P, PACK], I32)
-        nc.gpsimd.iota(
-            distance_i32[:], pattern=[[1, P], [-P, PACK]], base=3 * P, channel_multiplier=-1
-        )
-        distance = const.tile([P, P, PACK], F32)
-        nc.vector.tensor_copy(out=distance[:], in_=distance_i32[:])
-        causal = const.tile([P, P, PACK], F32)
-        nc.vector.tensor_single_scalar(out=causal[:], in_=distance[:], scalar=0.0, op=ALU.is_ge)
-        nc.vector.tensor_scalar_max(out=distance[:], in0=distance[:], scalar1=0.0)
-        amp = const.tile([P, H], F32)
-        nc.scalar.activation(out=amp[:], in_=amp_logit[:], func=ACT.Sigmoid)
-        log_amp = const.tile([P, H], F32)
-        nc.scalar.activation(out=log_amp[:], in_=amp[:], func=ACT.Ln)
-        decay = {}
-
-        def build_decay(h):
-            decay[h] = const.tile([P, P, PACK], F32, name="decay%d" % h)
-            nc.scalar.activation(
-                out=decay[h][:], in_=distance[:], func=ACT.Exp, scale=log_amp[:, h : h + 1]
-            )
-            nc.gpsimd.tensor_tensor(
-                out=decay[h][:], in0=decay[h][:], in1=causal[:], op=ALU.mult
-            )
-
-        build_decay(0)
-
         p_grouped = [
             const.tile([P, TILES, P, PACK], BF16, name="p_grouped%d" % r, align_bytes=64)
             for r in range(P_RING)
         ]
         for r in range(P_RING):
             nc.vector.memset(p_grouped[r][:].rearrange("p i j t -> p (i j t)").bitcast(I32), 0)
+
+        impulse = const.tile([P, L], F32)
+        nc.vector.memset(impulse[:, P:], 0.0)
+        nc.vector.tensor_copy(out=impulse[:, 0:P], in_=ident_f32[:])
+        amp = const.tile([P, H], F32)
+        nc.scalar.activation(out=amp[:], in_=amp_logit[:], func=ACT.Sigmoid)
+        decay = {}
+
+        powers = [const.tile([P, L], F32, name="powers%d" % h) for h in range(H)]
+        for h in range(H):
+            nc.vector.tensor_tensor_scan(
+                out=powers[h][:],
+                data0=amp[:, h : h + 1].to_broadcast([P, L]),
+                data1=impulse[:],
+                initial=0.0,
+                op0=ALU.mult,
+                op1=ALU.add,
+            )
+
+        def place_decay(h):
+            decay[h] = const.tile([P, P, PACK], F32, name="decay%d" % h)
+            nc.scalar.copy(
+                out=decay[h][:],
+                in_=powers[h][:].rearrange("p (a j) -> p j a", a=PACK)[:, :, ::-1],
+            )
 
         def flip_channels_last(rows_sb, name):
             words = rows_sb[:].bitcast(F32)
@@ -178,30 +177,35 @@ def tile_retention_pb_t_kernel(
             else:
                 nc.tensor.transpose(place, block, ident_bf16[:])
 
-        def score_matmul(unit, i, t, c, place):
+        def score_matmul(unit, i, count, t, c, place):
             nc.tensor.matmul(
                 out=place,
                 lhsT=flipped[unit]["k"][:, c * L + t * P : c * L + (t + 1) * P],
-                rhs=flipped[unit]["q"][:, c * L + i * P : c * L + (i + 1) * P],
+                rhs=flipped[unit]["q"][:, c * L + i * P : c * L + (i + count) * P],
                 start=(c == 0),
                 stop=(c == 1),
             )
 
-        def scores_and_flips(unit, tiles, who):
+        def scores_and_flips(unit, products, who):
             later = unit + FLIP_AHEAD
-            scores = psum.tile([P, TILES, P], F32, bufs=3)
-            matmuls = [(i, t, c, place) for place, (i, t) in enumerate(tiles) for c in range(2)]
+            scores = psum.tile([P, L], F32, bufs=3)
+            matmuls = []
+            column = 0
+            for i, count, t in products:
+                matmuls += [(i, count, t, c, scores[:, column : column + count * P]) for c in range(2)]
+                column += count * P
             if who is not None and later < UNITS:
                 bank = psum.tile([P, 2 * L], BF16, name="flipped_bank", bufs=2)
-                for n in range(2 * TILES):
+                flips = 2 * TILES
+                for n in range(flips):
                     flip_block(bank, later, who, n)
-                    if n < len(matmuls):
-                        i, t, c, place = matmuls[n]
-                        score_matmul(unit, i, t, c, scores[:, place, :])
+                    done, due = n * len(matmuls) // flips, (n + 1) * len(matmuls) // flips
+                    for matmul in matmuls[done:due]:
+                        score_matmul(unit, *matmul)
                 copy_flipped(bank, later, who)
             else:
-                for i, t, c, place in matmuls:
-                    score_matmul(unit, i, t, c, scores[:, place, :])
+                for matmul in matmuls:
+                    score_matmul(unit, *matmul)
             return scores
 
         def copy_flipped(bank, unit, who):
@@ -219,18 +223,18 @@ def tile_retention_pb_t_kernel(
             keys = i + 1
             nc.vector.tensor_tensor(
                 out=p_grouped[unit % P_RING][:, i, :, 0:keys],
-                in0=scores[:, place : place + keys, :].rearrange("p t j -> p j t"),
+                in0=scores[:, place * P : (place + keys) * P].rearrange("p (t j) -> p j t", t=keys),
                 in1=decay[unit % H][:, :, PACK - keys : PACK],
                 op=ALU.mult,
             )
 
         def first_query_tiles(unit):
-            scores = scores_and_flips(unit, [(0, 0), (1, 0), (1, 1)], "q")
+            scores = scores_and_flips(unit, [(0, 2, 0), (1, 1, 1)], "q")
             multiply_by_decay(unit, scores, 0, 0)
             multiply_by_decay(unit, scores, 1, 1)
 
         def query_tile(unit, i, who):
-            scores = scores_and_flips(unit, [(i, t) for t in range(i + 1)], who)
+            scores = scores_and_flips(unit, [(i, 1, t) for t in range(i + 1)], who)
             multiply_by_decay(unit, scores, 0, i)
 
         p_quantised = {}
@@ -271,6 +275,8 @@ def tile_retention_pb_t_kernel(
         for who in ("q", "k"):
             for unit in range(FLIP_AHEAD):
                 flip_in_a_row(unit, who)
+            if who == "q":
+                place_decay(0)
         outs_done = 0
         for unit in range(UNITS):
             b, h = divmod(unit, H)
@@ -308,7 +314,7 @@ def tile_retention_pb_t_kernel(
                 w_codes, w_scales = quantise(w_grouped[:], "w", 1)
                 x_quantised[0] = quantise(x_grouped[0][:], "x", 2)
             if unit + 1 < H:
-                build_decay(unit + 1)
+                place_decay(unit + 1)
         last = UNITS - 1
         quantise_p(last, 3, 1)
         for unit in range(outs_done, last):

@@ -58,16 +58,20 @@ def tile_retention_pb_t_kernel(
 
         amp_logit = const.tile([P, H], BF16)
         nc.scalar.dma_start(out=amp_logit[:], in_=amplitude.partition_broadcast(P))
+        bias_row = const.tile([P, DIM], BF16)
+        nc.vector.memset(bias_row[:].bitcast(I32), 0)
+        nc.scalar.dma_start(out=bias_row[0:1, :], in_=wv_b.unsqueeze(0))
+        ones = const.tile([P, P], BF16)
+        bias = const.tile([P, DIM], F32)
         load_batch(0)
         w_sb = load_rows(const, "w_sb", wv_w)
-        bias = const.tile([P, DIM], BF16)
-        nc.sync.dma_start(out=bias[:], in_=wv_b.partition_broadcast(P))
         load_batch(1)
 
         ident_bf16 = const.tile([P, P], BF16)
         make_identity(nc, ident_bf16[:])
         ident_f32 = const.tile([P, P], F32)
         make_identity(nc, ident_f32[:])
+        nc.gpsimd.memset(ones[:], 1.0)
         minus_ident = const.tile([P, P], BF16)
         nc.vector.tensor_scalar_mul(out=minus_ident[:], in0=ident_bf16[:], scalar1=-1.0)
 
@@ -308,13 +312,18 @@ def tile_retention_pb_t_kernel(
                 quantise_p(unit, 0, 2)
                 quantise_p(unit, 2, 1)
             query_tile(unit, 3, None)
+            if unit + 1 < H:
+                place_decay(unit + 1)
             if unit == 0:
+                bias_bank = psum.tile([P, L], F32, name="shared_bank", bufs=3)
+                nc.tensor.matmul(
+                    out=bias_bank[:], lhsT=ones[:], rhs=bias_row[:], start=True, stop=True
+                )
+                nc.scalar.copy(out=bias[:], in_=bias_bank[:])
                 w_grouped = flip_channels_last(w_sb, "w")
                 x_grouped[0] = flip_channels_last(loaded[0]["x"], "x")
                 w_codes, w_scales = quantise(w_grouped[:], "w", 1)
                 x_quantised[0] = quantise(x_grouped[0][:], "x", 2)
-            if unit + 1 < H:
-                place_decay(unit + 1)
         last = UNITS - 1
         quantise_p(last, 3, 1)
         for unit in range(outs_done, last):

from contextlib import ExitStack

import concourse.mybir as mybir
from concourse.masks import make_identity

BF16 = mybir.dt.bfloat16
F32 = mybir.dt.float32
I32 = mybir.dt.int32
U32 = mybir.dt.uint32
U8 = mybir.dt.uint8
FP8X4 = mybir.dt.float8_e4m3fn_x4
ALU = mybir.AluOpType
ACT = mybir.ActivationFunctionType

B, L, H, D = 8, 512, 4, 128
DIM = H * D
P = 128
PACK = 4
TILES = L // P
UNITS = B * H
P_RING = 3
OUT_LAG = 3
END_LAG = 2
FLIP_AHEAD = 2

FLOPS = 2 * B * L * DIM * DIM + 3 * 2 * B * H * L * L * D


def tile_retention_pb_t_kernel(
    tc, q_rot_re, q_rot_im, k_rot_re, k_rot_im, x, wv_w, wv_b, amplitude, out
):
    nc = tc.nc
    with ExitStack() as ctx:
        ctx.enter_context(tc.manual_schedule())
        const = ctx.enter_context(tc.tile_pool(name="const", bufs=1))
        inputs = ctx.enter_context(tc.tile_pool(name="inputs", bufs=3))
        work = ctx.enter_context(tc.tile_pool(name="work", bufs=2))
        psum = ctx.enter_context(tc.psum_pool(name="psum", bufs=1))

        def load_rows(pool, name, rows):
            rows_sb = pool.tile([P, TILES * DIM], BF16, name=name)
            nc.sync.dma_start(
                out=rows_sb[:].rearrange("p (i c) -> p i c", i=TILES),
                in_=rows.rearrange("(i p) c -> p i c", p=P),
            )
            return rows_sb

        loaded = {}

        def load_batch(b):
            loaded[b] = {
                "q_re": load_rows(inputs, "q_re_sb", q_rot_re[b].rearrange("l h d -> l (h d)")),
                "q_im": load_rows(inputs, "q_im_sb", q_rot_im[b].rearrange("l h d -> l (h d)")),
                "k_re": load_rows(inputs, "k_re_sb", k_rot_re[b].rearrange("l h d -> l (h d)")),
                "k_im": load_rows(inputs, "k_im_sb", k_rot_im[b].rearrange("l h d -> l (h d)")),
                "x": load_rows(inputs, "x_sb", x[b]),
            }

        amp_logit = const.tile([P, H], BF16)
        nc.scalar.dma_start(out=amp_logit[:], in_=amplitude.partition_broadcast(P))
        bias_row = const.tile([P, DIM], BF16)
        nc.vector.memset(bias_row[:].bitcast(I32), 0)
        nc.scalar.dma_start(out=bias_row[0:1, :], in_=wv_b.unsqueeze(0))
        ones = const.tile([P, P], BF16)
        bias = const.tile([P, DIM], F32)
        load_batch(0)
        w_sb = load_rows(const, "w_sb", wv_w)
        load_batch(1)

        ident_bf16 = const.tile([P, P], BF16)
        make_identity(nc, ident_bf16[:])
        ident_f32 = const.tile([P, P], F32)
        make_identity(nc, ident_f32[:])
        nc.gpsimd.memset(ones[:], 1.0)
        minus_ident = const.tile([P, P], BF16)
        nc.vector.tensor_scalar_mul(out=minus_ident[:], in0=ident_bf16[:], scalar1=-1.0)

        p_grouped = [
            const.tile([P, TILES, P, PACK], BF16, name="p_grouped%d" % r, align_bytes=64)
            for r in range(P_RING)
        ]
        for r in range(P_RING):
            nc.vector.memset(p_grouped[r][:].rearrange("p i j t -> p (i j t)").bitcast(I32), 0)

        impulse = const.tile([P, L], F32)
        nc.vector.memset(impulse[:, P:], 0.0)
        nc.vector.tensor_copy(out=impulse[:, 0:P], in_=ident_f32[:])
        amp = const.tile([P, H], F32)
        nc.scalar.activation(out=amp[:], in_=amp_logit[:], func=ACT.Sigmoid)
        decay = {}

        powers = [const.tile([P, L], F32, name="powers%d" % h) for h in range(H)]
        for h in range(H):
            nc.vector.tensor_tensor_scan(
                out=powers[h][:],
                data0=amp[:, h : h + 1].to_broadcast([P, L]),
                data1=impulse[:],
                initial=0.0,
                op0=ALU.mult,
                op1=ALU.add,
            )

        def place_decay(h):
            decay[h] = const.tile([P, P, PACK], F32, name="decay%d" % h)
            nc.scalar.copy(
                out=decay[h][:],
                in_=powers[h][:].rearrange("p (a j) -> p j a", a=PACK)[:, :, ::-1],
            )

        def flip_channels_last(rows_sb, name):
            words = rows_sb[:].bitcast(F32)
            grouped = work.tile([P, L * PACK], BF16, name=name + "_grouped", align_bytes=64)
            grouped_words = grouped[:].bitcast(F32).rearrange("p (r u) -> p r u", u=2)
            for half in range(2):
                bank = psum.tile([P, 2, 2 * P], F32, name="shared_bank", bufs=3)
                for i in range(2):
                    for u in range(2):
                        first = (2 * half + i) * 2 * P + u * P
                        nc.tensor.transpose(
                            bank[:, u, i * P : (i + 1) * P],
                            words[:, first : first + P],
                            ident_f32[:],
                        )
                nc.scalar.copy(
                    out=grouped_words[:, half * 2 * P : (half + 1) * 2 * P, :],
                    in_=bank[:].rearrange("p u r -> p r u"),
                )
            return grouped

        def quantise(grouped_flat, name, bufs):
            columns = grouped_flat.shape[1] // PACK
            codes = work.tile([P, columns], U32, name=name + "_codes", bufs=bufs, align_bytes=64)
            scales = work.tile([P, columns], U8, name=name + "_scales", bufs=bufs, align_bytes=64)
            nc.vector.quantize_mx(out=codes[:].bitcast(FP8X4), scales=scales[:], in_=grouped_flat)
            return codes, scales

        x_grouped = {}
        x_quantised = {}
        v_grouped = {}
        v_quantised = {}

        def project_values(unit):
            b, h = divmod(unit, H)
            x_codes, x_scales = x_quantised[b]
            v_acc = psum.tile([P, TILES, D], F32, name="shared_bank", bufs=3)
            for t in range(TILES):
                nc.tensor.matmul_mx(
                    out=v_acc[:, t, :],
                    lhsT=x_codes[:, t * P : (t + 1) * P].bitcast(FP8X4),
                    lhsT_scale=x_scales[:, t * P : (t + 1) * P],
                    rhs=w_codes[:, h * D : (h + 1) * D].bitcast(FP8X4),
                    rhs_scale=w_scales[:, h * D : (h + 1) * D],
                    start=True,
                    stop=True,
                )
            v_sums = work.tile([P, D, PACK], F32, bufs=3)
            nc.scalar.copy(out=v_sums[:], in_=v_acc[:].rearrange("p t d -> p d t"))
            v_grouped[unit] = work.tile([P, D, PACK], BF16, name="v_grouped", bufs=4, align_bytes=64)
            nc.gpsimd.tensor_tensor(
                out=v_grouped[unit][:],
                in0=v_sums[:],
                in1=bias[:, h * D : (h + 1) * D].unsqueeze(2).to_broadcast([P, D, PACK]),
                op=ALU.add,
            )

        def quantise_values(unit):
            v_quantised[unit] = quantise(
                v_grouped[unit][:].rearrange("p d t -> p (d t)"), "v", OUT_LAG + 2
            )

        flipped = {}

        def flip_block(bank, unit, who, n):
            b, h = divmod(unit, H)
            c, i = divmod(n, TILES)
            rows_sb = loaded[b][who + ("_re", "_im")[c]]
            block = rows_sb[:, i * DIM + h * D : i * DIM + (h + 1) * D]
            place = bank[:, n * P : (n + 1) * P]
            if who == "k" and c == 1:
                nc.tensor.matmul(out=place, lhsT=block, rhs=minus_ident[:], start=True, stop=True)
            else:
                nc.tensor.transpose(place, block, ident_bf16[:])

        def score_matmul(unit, i, count, t, c, place):
            nc.tensor.matmul(
                out=place,
                lhsT=flipped[unit]["k"][:, c * L + t * P : c * L + (t + 1) * P],
                rhs=flipped[unit]["q"][:, c * L + i * P : c * L + (i + count) * P],
                start=(c == 0),
                stop=(c == 1),
            )

        def scores_and_flips(unit, products, who):
            later = unit + FLIP_AHEAD
            scores = psum.tile([P, L], F32, bufs=3)
            matmuls = []
            column = 0
            for i, count, t in products:
                matmuls += [(i, count, t, c, scores[:, column : column + count * P]) for c in range(2)]
                column += count * P
            if who is not None and later < UNITS:
                bank = psum.tile([P, 2 * L], BF16, name="flipped_bank", bufs=2)
                flips = 2 * TILES
                for n in range(flips):
                    flip_block(bank, later, who, n)
                    done, due = n * len(matmuls) // flips, (n + 1) * len(matmuls) // flips
                    for matmul in matmuls[done:due]:
                        score_matmul(unit, *matmul)
                copy_flipped(bank, later, who)
            else:
                for matmul in matmuls:
                    score_matmul(unit, *matmul)
            return scores

        def copy_flipped(bank, unit, who):
            flipped_sb = work.tile([P, 2 * L], BF16, name=who + "_flipped", bufs=FLIP_AHEAD + 1)
            nc.scalar.copy(out=flipped_sb[:].bitcast(F32), in_=bank[:].bitcast(F32))
            flipped[unit][who] = flipped_sb

        def flip_in_a_row(unit, who):
            bank = psum.tile([P, 2 * L], BF16, name="flipped_bank", bufs=2)
            for n in range(2 * TILES):
                flip_block(bank, unit, who, n)
            copy_flipped(bank, unit, who)

        def multiply_by_decay(unit, scores, place, i):
            keys = i + 1
            nc.vector.tensor_tensor(
                out=p_grouped[unit % P_RING][:, i, :, 0:keys],
                in0=scores[:, place * P : (place + keys) * P].rearrange("p (t j) -> p j t", t=keys),
                in1=decay[unit % H][:, :, PACK - keys : PACK],
                op=ALU.mult,
            )

        def first_query_tiles(unit):
            scores = scores_and_flips(unit, [(0, 2, 0), (1, 1, 1)], "q")
            multiply_by_decay(unit, scores, 0, 0)
            multiply_by_decay(unit, scores, 1, 1)

        def query_tile(unit, i, who):
            scores = scores_and_flips(unit, [(i, 1, t) for t in range(i + 1)], who)
            multiply_by_decay(unit, scores, 0, i)

        p_quantised = {}

        def quantise_p(unit, first=0, count=TILES):
            grouped = p_grouped[unit % P_RING][:, first : first + count, :, :]
            name, bufs = ("p", OUT_LAG + 1) if count == TILES else ("p_from%d" % first, 1)
            codes, scales = quantise(grouped.rearrange("p i j t -> p (i j t)"), name, bufs)
            for n in range(count):
                columns = slice(n * P, (n + 1) * P)
                p_quantised[unit, first + n] = (codes[:, columns], scales[:, columns])

        def weighted_values(unit, first=0, count=TILES, copy=nc.scalar.copy):
            b, h = divmod(unit, H)
            v_codes, v_scales = v_quantised[unit]
            o_acc = psum.tile([P, TILES, D], F32, name="shared_bank", bufs=3)
            for i in range(first, first + count):
                p_codes, p_scales = p_quantised[unit, i]
                nc.tensor.matmul_mx(
                    out=o_acc[:, i, :],
                    lhsT=p_codes.bitcast(FP8X4),
                    lhsT_scale=p_scales,
                    rhs=v_codes[:].bitcast(FP8X4),
                    rhs_scale=v_scales[:],
                    start=True,
                    stop=True,
                )
            tiles = slice(first, first + count)
            out_sb = work.tile([P, TILES, D], F32, bufs=3)
            copy(out=out_sb[:, tiles, :], in_=o_acc[:, tiles, :])
            nc.sync.dma_start(
                out=out[b].rearrange("(i p) c -> p i c", p=P)[:, tiles, h * D : (h + 1) * D],
                in_=out_sb[:, tiles, :],
            )

        for unit in range(UNITS):
            flipped[unit] = {}
        for who in ("q", "k"):
            for unit in range(FLIP_AHEAD):
                flip_in_a_row(unit, who)
            if who == "q":
                place_decay(0)
        outs_done = 0
        for unit in range(UNITS):
            b, h = divmod(unit, H)
            if h == 0 and b + 2 < B:
                load_batch(b + 2)
            if h == H - 2 and b + 1 < B:
                x_grouped[b + 1] = flip_channels_last(loaded[b + 1]["x"], "x")
            first_query_tiles(unit)
            query_tile(unit, 2, "k")
            lag = OUT_LAG if unit + FLIP_AHEAD < UNITS else END_LAG
            for ready in range(outs_done, unit - lag + 1):
                weighted_values(ready)
            outs_done = max(outs_done, unit - lag + 1)
            if unit == 1:
                project_values(0)
                project_values(1)
            if 1 <= unit < UNITS - 1:
                project_values(unit + 1)
            if unit >= 1:
                quantise_p(unit - 1)
            if unit == 2:
                quantise_values(0)
                quantise_values(1)
            if unit >= 2:
                quantise_values(unit)
            if h == H - 2 and b + 1 < B:
                x_quantised[b + 1] = quantise(x_grouped[b + 1][:], "x", 2)
            if unit == UNITS - 1:
                quantise_p(unit, 0, 2)
                quantise_p(unit, 2, 1)
            query_tile(unit, 3, None)
            if unit + 1 < H:
                place_decay(unit + 1)
            if unit == 0:
                bias_bank = psum.tile([P, L], F32, name="shared_bank", bufs=3)
                nc.tensor.matmul(
                    out=bias_bank[:], lhsT=ones[:], rhs=bias_row[:], start=True, stop=True
                )
                nc.scalar.copy(out=bias[:], in_=bias_bank[:])
                w_grouped = flip_channels_last(w_sb, "w")
                x_grouped[0] = flip_channels_last(loaded[0]["x"], "x")
                w_codes, w_scales = quantise(w_grouped[:], "w", 1)
                x_quantised[0] = quantise(x_grouped[0][:], "x", 2)
        last = UNITS - 1
        quantise_p(last, 3, 1)
        for unit in range(outs_done, last):
            weighted_values(unit)
        weighted_values(last, 0, 3)
        weighted_values(last, 3, 1, nc.vector.tensor_copy)
